import numpy as np
import ml_dtypes


def mxq(x, axis, fmt="e4m3"):
    dtype, down = {"e4m3": (ml_dtypes.float8_e4m3fn, 7), "e5m2": (ml_dtypes.float8_e5m2, 14)}[fmt]
    v = np.moveaxis(np.asarray(x, np.float32).astype(ml_dtypes.bfloat16).astype(np.float64), axis, -1)
    blocks = v.reshape(v.shape[:-1] + (-1, 32))
    amax = np.abs(blocks).max(-1, keepdims=True)
    byte = np.maximum(np.where(amax > 0, np.frexp(amax)[1] - 1 + 127, 0) - down, 1)
    scale = np.exp2(byte - 127.0)
    codes = (blocks / scale).astype(np.float32).astype(dtype).astype(np.float64)
    return np.moveaxis((codes * scale).reshape(v.shape), -1, axis)


WIDE = False


def mx_kscale(k):
    if not WIDE:
        return np.ones(k)
    levels = np.array([10, -10, 5, -5, 0])
    a = np.random.permutation(np.resize(levels, k // 512 * 4)).reshape(k // 512, 4)
    idx = np.arange(k)
    return np.exp2(a[idx // 512, idx % 128 // 32])


BF16 = ml_dtypes.bfloat16


def bf(x):
    return np.asarray(x, np.float32).astype(BF16)


def f64(x):
    return np.asarray(x).astype(np.float64)


B, T, E, H, FF = 4, 1024, 1024, 8, 512
EPS = 1e-5


def layernorm(r, g):
    mu = r.mean(-1, keepdims=True)
    var = ((r - mu) ** 2).mean(-1, keepdims=True)
    return (r - mu) / np.sqrt(var + EPS) * g


def setup_inputs():
    t = mx_kscale(FF)
    z = np.random.standard_normal((B, T, FF))
    return {
        "y_act": bf(z * z / (1.0 + np.exp(-z)) * t),
        "h": bf(np.random.standard_normal((B, T, E))),
        "W2": bf(np.random.standard_normal((FF, E)) / np.sqrt(FF) / t[:, None]),
        "b2": bf(np.random.standard_normal(E) * 0.1),
        "g2": bf(1.0 + np.random.standard_normal(E) * 0.1),
    }


def reference(y_act, h, W2, b2, g2):
    ff = (mxq(f64(y_act), 2, "e4m3") @ mxq(f64(W2), 0, "e4m3")) + f64(b2)
    return layernorm(ff + f64(h), f64(g2))

@@ -1,0 +1,239 @@
+from contextlib import ExitStack
+
+import concourse.mybir as mybir
+from concourse.masks import make_identity
+
+F32 = mybir.dt.float32
+BF16 = mybir.dt.bfloat16
+U32 = mybir.dt.uint32
+U8 = mybir.dt.uint8
+FP8X4 = mybir.dt.float8_e4m3fn_x4
+ALU = mybir.AluOpType
+ACT = mybir.ActivationFunctionType
+
+P = 128
+PACK = 4
+TOKENS = 4 * 1024
+K = 512
+E = 1024
+EPS = 1e-5
+BANK = 512
+BANKS = E // BANK
+N_TILES = TOKENS // P
+GROUP = 4
+N_GROUPS = N_TILES // GROUP
+PAIR = 2
+WORDS = K // 2
+LOADS_AHEAD = 3
+
+FLOPS = 2 * TOKENS * K * E
+
+
+def tile_transformerblock_pb_t_kernel(tc, y_act, h, W2, b2, g2, out):
+    nc = tc.nc
+    y_groups = y_act.flatten_outer_dims().rearrange("(g p t) k -> g p (t k)", p=P, t=GROUP)
+    h_groups = h.flatten_outer_dims().rearrange("(g p t) e -> g p (t e)", p=P, t=GROUP)
+    out_groups = out.flatten_outer_dims().rearrange("(g p t) e -> g p t e", p=P, t=GROUP)
+    bank_cols = [slice(c * BANK, (c + 1) * BANK) for c in range(BANKS)]
+
+    with ExitStack() as ctx:
+        consts = ctx.enter_context(tc.tile_pool(name="consts", bufs=1))
+        loads = ctx.enter_context(tc.tile_pool(name="loads", bufs=LOADS_AHEAD))
+        operand = ctx.enter_context(tc.tile_pool(name="operand", bufs=3))
+        rows = ctx.enter_context(tc.tile_pool(name="rows", bufs=6))
+        stats = ctx.enter_context(tc.tile_pool(name="stats", bufs=8))
+        gain_psum = ctx.enter_context(tc.psum_pool(name="gain_psum", bufs=1))
+        acc_psum = ctx.enter_context(tc.psum_pool(name="acc_psum", bufs=2))
+        xt_psum = ctx.enter_context(tc.psum_pool(name="xt_psum", bufs=2))
+        ctx.enter_context(tc.manual_schedule())
+
+        y_sb, h_sb = {}, {}
+        xt_of, grouped_of, codes_of, scales_of = {}, {}, {}, {}
+        acc_of, resid_of, scaled_of = {}, {}, {}
+        sums_of, negmean_of, sumsq_of, std_of, rstd_of = {}, {}, {}, {}, {}
+
+        def load_group(g):
+            y_t = loads.tile([P, GROUP * K], BF16)
+            nc.sync.dma_start(out=y_t[:], in_=y_groups[g])
+            h_t = loads.tile([P, GROUP * E], BF16)
+            nc.sync.dma_start(out=h_t[:], in_=h_groups[g])
+            y_sb[g], h_sb[g] = y_t, h_t
+
+        vec_rows = consts.tile([P, 2, E], BF16)
+        nc.vector.memset(vec_rows[:], 0.0)
+        nc.sync.dma_start(out=vec_rows[0:1, 0, :], in_=b2.unsqueeze(0))
+        nc.sync.dma_start(out=vec_rows[0:1, 1, :], in_=g2.unsqueeze(0))
+        w_raw = consts.tile([P, PACK, E], BF16)
+        nc.sync.dma_start(
+            out=w_raw[:].rearrange("p (u e) c -> p u (e c)", e=2),
+            in_=W2.rearrange("(u q e) c -> q u (e c)", u=2, e=2),
+        )
+        for g in range(LOADS_AHEAD):
+            load_group(g)
+
+        ones = consts.tile([P, P], BF16)
+        nc.vector.memset(ones[:], 1.0)
+        eps_col = consts.tile([P, 1], F32)
+        nc.vector.memset(eps_col[:], EPS)
+        table_warm = consts.tile([P, 1], F32)
+        nc.scalar.activation(out=table_warm[:], in_=eps_col[:], func=ACT.Sqrt)
+        ident = consts.tile([P, P], F32)
+        make_identity(nc, ident[:])
+
+        bias_bc = consts.tile([P, E], F32)
+        gain_bc = []
+        for c in range(BANKS):
+            bias_ps = acc_psum.tile([P, BANK], F32, tag="acc%d" % c)
+            nc.tensor.matmul(out=bias_ps[:], lhsT=ones[:], rhs=vec_rows[:, 0, bank_cols[c]], start=True, stop=True)
+            nc.scalar.copy(out=bias_bc[:, bank_cols[c]], in_=bias_ps[:])
+            gain_ps = gain_psum.tile([P, BANK], F32, tag="gain%d" % c)
+            nc.tensor.matmul(out=gain_ps[:], lhsT=ones[:], rhs=vec_rows[:, 1, bank_cols[c]], start=True, stop=True)
+            gain_bc.append(gain_ps)
+
+        w_grouped = consts.tile([P, E, PACK], BF16, align_bytes=64)
+        w_codes = consts.tile([P, E], U32, align_bytes=64)
+        w_scales = consts.tile([P, E], U8, align_bytes=64)
+        nc.vector.tensor_copy(
+            out=w_grouped[:, bank_cols[0], :].rearrange("p (c i) t -> p c t i", i=4),
+            in_=w_raw[:, :, bank_cols[0]].rearrange("p t (c i) -> p c t i", i=4),
+        )
+        nc.scalar.copy(
+            out=w_grouped[:, bank_cols[1], :].rearrange("p (c i) t -> p c t i", i=4),
+            in_=w_raw[:, :, bank_cols[1]].rearrange("p t (c i) -> p c t i", i=4),
+        )
+        for c in range(BANKS):
+            nc.vector.quantize_mx(
+                out=w_codes[:, bank_cols[c]].bitcast(FP8X4),
+                scales=w_scales[:, bank_cols[c]],
+                in_=w_grouped[:, bank_cols[c], :].rearrange("p c t -> p (c t)"),
+            )
+
+        def transpose_pair(j):
+            y_words = y_sb[PAIR * j // GROUP][:].bitcast(F32)
+            xt = xt_psum.tile([P, PAIR * 2, P], F32)
+            for a in range(PAIR):
+                t = (PAIR * j + a) % GROUP
+                for u in range(2):
+                    first = t * WORDS + u * P
+                    nc.tensor.transpose(xt[:, 2 * a + u, :], y_words[:, first : first + P], ident[:])
+            xt_of[j] = xt
+
+        def regroup_pair(j):
+            grouped = operand.tile([P, PAIR * P * PACK], BF16, align_bytes=64)
+            nc.scalar.copy(
+                out=grouped[:].bitcast(F32).rearrange("p (a r u) -> p a r u", a=PAIR, u=2),
+                in_=xt_of[j][:].rearrange("p (a u) r -> p a r u", u=2),
+            )
+            grouped_of[j] = grouped
+
+        def quantise_pair(j):
+            y_codes = operand.tile([P, PAIR * P], U32, align_bytes=64)
+            y_scales = operand.tile([P, PAIR * P], U8, align_bytes=64)
+            nc.vector.quantize_mx(out=y_codes[:].bitcast(FP8X4), scales=y_scales[:], in_=grouped_of[j][:])
+            codes_of[j], scales_of[j] = y_codes, y_scales
+
+        def add_bias(i):
+            resid = rows.tile([P, E], F32)
+            t = i % GROUP
+            nc.gpsimd.tensor_tensor(
+                out=resid[:], in0=h_sb[i // GROUP][:, t * E : (t + 1) * E], in1=bias_bc[:], op=ALU.add
+            )
+            resid_of[i] = resid
+
+        def multiply(i):
+            tokens = slice((i % PAIR) * P, (i % PAIR + 1) * P)
+            acc_of[i] = []
+            for c in range(BANKS):
+                acc = acc_psum.tile([P, BANK], F32, tag="acc%d" % c)
+                nc.tensor.matmul_mx(
+                    out=acc[:],
+                    lhsT=codes_of[i // PAIR][:, tokens].bitcast(FP8X4),
+                    lhsT_scale=scales_of[i // PAIR][:, tokens],
+                    rhs=w_codes[:, bank_cols[c]].bitcast(FP8X4),
+                    rhs_scale=w_scales[:, bank_cols[c]],
+                    start=True,
+                    stop=True,
+                )
+                acc_of[i].append(acc)
+
+        def add_product(i):
+            sums = stats.tile([P, BANKS], F32)
+            for c, acc in enumerate(acc_of[i]):
+                nc.vector.scalar_tensor_tensor(
+                    out=resid_of[i][:, bank_cols[c]],
+                    in0=acc[:],
+                    scalar=0.0,
+                    in1=resid_of[i][:, bank_cols[c]],
+                    op0=ALU.add,
+                    op1=ALU.add,
+                    accum_out=sums[:, c : c + 1],
+                )
+            sums_of[i] = sums
+
+        def negative_mean(i):
+            negmean = stats.tile([P, 1], F32)
+            sums = sums_of[i]
+            nc.vector.tensor_scalar(
+                out=negmean[:], in0=sums[:, 0:1], scalar1=sums[:, 1:2], scalar2=-1.0 / E, op0=ALU.add, op1=ALU.mult
+            )
+            negmean_of[i] = negmean
+
+        def sum_squares(i):
+            squares = rows.tile([P, E], BF16, bufs=2)
+            sumsq = stats.tile([P, 1], F32)
+            nc.scalar.activation(
+                out=squares[:], in_=resid_of[i][:], func=ACT.Square, bias=negmean_of[i][:], scale=1.0, accum_out=sumsq[:]
+            )
+            sumsq_of[i] = sumsq
+
+        def centre_and_gain(i):
+            scaled = rows.tile([P, E], F32)
+            for c in range(BANKS):
+                nc.vector.scalar_tensor_tensor(
+                    out=scaled[:, bank_cols[c]],
+                    in0=resid_of[i][:, bank_cols[c]],
+                    scalar=negmean_of[i][:],
+                    in1=gain_bc[c][:],
+                    op0=ALU.add,
+                    op1=ALU.mult,
+                )
+            scaled_of[i] = scaled
+
+        def standard_deviation(i):
+            std = stats.tile([P, 1], F32)
+            nc.scalar.activation(out=std[:], in_=sumsq_of[i][:], func=ACT.Sqrt, bias=eps_col[:], scale=1.0 / E)
+            std_of[i] = std
+
+        def reciprocal(i):
+            rstd = stats.tile([P, 1], F32)
+            nc.vector.reciprocal(out=rstd[:], in_=std_of[i][:])
+            rstd_of[i] = rstd
+
+        def normalise_and_store(i):
+            scaled = scaled_of[i]
+            nc.scalar.activation(out=scaled[:], in_=scaled[:], func=ACT.Copy, scale=rstd_of[i][:])
+            nc.sync.dma_start(out=out_groups[i // GROUP][:, i % GROUP, :], in_=scaled[:])
+
+        def if_tile(stage, i):
+            if 0 <= i < N_TILES:
+                stage(i)
+
+        def if_first_of_pair(stage, i):
+            if 0 <= i < N_TILES and i % PAIR == 0:
+                stage(i // PAIR)
+
+        for s in range(-4, N_TILES + 3):
+            if_first_of_pair(transpose_pair, s + 4)
+            if_tile(add_bias, s + 3)
+            if_tile(multiply, s + 1)
+            if_tile(add_product, s)
+            if_first_of_pair(quantise_pair, s + 3)
+            if_tile(centre_and_gain, s - 1)
+            if_tile(negative_mean, s)
+            if_tile(reciprocal, s - 2)
+            if_tile(sum_squares, s - 1)
+            if_tile(normalise_and_store, s - 3)
+            if_tile(standard_deviation, s - 1)
+            if_first_of_pair(regroup_pair, s + 4)
+            if s > 0 and s % GROUP == 1 and s // GROUP + LOADS_AHEAD < N_GROUPS:
+                load_group(s // GROUP + LOADS_AHEAD)

@@ -161,9 +161,9 @@ def tile_transformerblock_pb_t_kernel(tc, y_act, h, W2, b2, g2, out):
             for c, acc in enumerate(acc_of[i]):
                 nc.vector.scalar_tensor_tensor(
                     out=resid_of[i][:, bank_cols[c]],
-                    in0=acc[:],
+                    in0=resid_of[i][:, bank_cols[c]],
                     scalar=0.0,
-                    in1=resid_of[i][:, bank_cols[c]],
+                    in1=acc[:],
                     op0=ALU.add,
                     op1=ALU.add,
                     accum_out=sums[:, c : c + 1],

@@ -25,6 +25,7 @@ N_GROUPS = N_TILES // GROUP
 PAIR = 2
 WORDS = K // 2
 LOADS_AHEAD = 3
+GPSIMD_COLS = 768
 
 FLOPS = 2 * TOKENS * K * E
 
@@ -44,7 +45,7 @@ def tile_transformerblock_pb_t_kernel(tc, y_act, h, W2, b2, g2, out):
         stats = ctx.enter_context(tc.tile_pool(name="stats", bufs=8))
         gain_psum = ctx.enter_context(tc.psum_pool(name="gain_psum", bufs=1))
         acc_psum = ctx.enter_context(tc.psum_pool(name="acc_psum", bufs=2))
-        xt_psum = ctx.enter_context(tc.psum_pool(name="xt_psum", bufs=2))
+        xt_psum = ctx.enter_context(tc.psum_pool(name="xt_psum", bufs=1))
         ctx.enter_context(tc.manual_schedule())
 
         y_sb, h_sb = {}, {}
@@ -80,12 +81,18 @@ def tile_transformerblock_pb_t_kernel(tc, y_act, h, W2, b2, g2, out):
         ident = consts.tile([P, P], F32)
         make_identity(nc, ident[:])
 
-        bias_bc = consts.tile([P, E], F32)
+        bias_bc = consts.tile([P, GPSIMD_COLS], F32)
+        bias_tail = gain_psum.tile([P, E - GPSIMD_COLS], F32)
+        nc.tensor.matmul(out=bias_tail[:], lhsT=ones[:], rhs=vec_rows[:, 0, GPSIMD_COLS:E], start=True, stop=True)
         gain_bc = []
         for c in range(BANKS):
+            first = c * BANK
+            width = min(BANK, GPSIMD_COLS - first)
             bias_ps = acc_psum.tile([P, BANK], F32, tag="acc%d" % c)
-            nc.tensor.matmul(out=bias_ps[:], lhsT=ones[:], rhs=vec_rows[:, 0, bank_cols[c]], start=True, stop=True)
-            nc.scalar.copy(out=bias_bc[:, bank_cols[c]], in_=bias_ps[:])
+            nc.tensor.matmul(
+                out=bias_ps[:, :width], lhsT=ones[:], rhs=vec_rows[:, 0, first : first + width], start=True, stop=True
+            )
+            nc.scalar.copy(out=bias_bc[:, first : first + width], in_=bias_ps[:, :width])
             gain_ps = gain_psum.tile([P, BANK], F32, tag="gain%d" % c)
             nc.tensor.matmul(out=gain_ps[:], lhsT=ones[:], rhs=vec_rows[:, 1, bank_cols[c]], start=True, stop=True)
             gain_bc.append(gain_ps)
@@ -134,11 +141,23 @@ def tile_transformerblock_pb_t_kernel(tc, y_act, h, W2, b2, g2, out):
 
         def add_bias(i):
             resid = rows.tile([P, E], F32)
-            t = i % GROUP
+            first = (i % GROUP) * E
             nc.gpsimd.tensor_tensor(
-                out=resid[:], in0=h_sb[i // GROUP][:, t * E : (t + 1) * E], in1=bias_bc[:], op=ALU.add
+                out=resid[:, :GPSIMD_COLS],
+                in0=h_sb[i // GROUP][:, first : first + GPSIMD_COLS],
+                in1=bias_bc[:],
+                op=ALU.add,
             )
             resid_of[i] = resid
+
+        def add_bias_tail(i):
+            first = (i % GROUP) * E
+            nc.vector.tensor_tensor(
+                out=resid_of[i][:, GPSIMD_COLS:],
+                in0=h_sb[i // GROUP][:, first + GPSIMD_COLS : first + E],
+                in1=bias_tail[:],
+                op=ALU.add,
+            )
 
         def multiply(i):
             tokens = slice((i % PAIR) * P, (i % PAIR + 1) * P)
@@ -227,6 +246,7 @@ def tile_transformerblock_pb_t_kernel(tc, y_act, h, W2, b2, g2, out):
             if_tile(add_bias, s + 3)
             if_tile(multiply, s + 1)
             if_tile(add_product, s)
+            if_tile(add_bias_tail, s + 1)
             if_first_of_pair(quantise_pair, s + 3)
             if_tile(centre_and_gain, s - 1)
             if_tile(negative_mean, s)
@@ -235,5 +255,5 @@ def tile_transformerblock_pb_t_kernel(tc, y_act, h, W2, b2, g2, out):
             if_tile(normalise_and_store, s - 3)
             if_tile(standard_deviation, s - 1)
             if_first_of_pair(regroup_pair, s + 4)
-            if s > 0 and s % GROUP == 1 and s // GROUP + LOADS_AHEAD < N_GROUPS:
+            if s > 0 and s % GROUP == GROUP - 1 and s // GROUP + LOADS_AHEAD < N_GROUPS:
                 load_group(s // GROUP + LOADS_AHEAD)

@@ -25,7 +25,7 @@ N_GROUPS = N_TILES // GROUP
 PAIR = 2
 WORDS = K // 2
 LOADS_AHEAD = 3
-GPSIMD_COLS = 768
+GPSIMD_COLS = 896
 
 FLOPS = 2 * TOKENS * K * E
 
@@ -82,16 +82,14 @@ def tile_transformerblock_pb_t_kernel(tc, y_act, h, W2, b2, g2, out):
         make_identity(nc, ident[:])
 
         bias_bc = consts.tile([P, GPSIMD_COLS], F32)
-        bias_tail = gain_psum.tile([P, E - GPSIMD_COLS], F32)
-        nc.tensor.matmul(out=bias_tail[:], lhsT=ones[:], rhs=vec_rows[:, 0, GPSIMD_COLS:E], start=True, stop=True)
+        bias_last_bank = gain_psum.tile([P, BANK], F32)
+        nc.tensor.matmul(out=bias_last_bank[:], lhsT=ones[:], rhs=vec_rows[:, 0, E - BANK : E], start=True, stop=True)
         gain_bc = []
         for c in range(BANKS):
             first = c * BANK
             width = min(BANK, GPSIMD_COLS - first)
             bias_ps = acc_psum.tile([P, BANK], F32, tag="acc%d" % c)
-            nc.tensor.matmul(
-                out=bias_ps[:, :width], lhsT=ones[:], rhs=vec_rows[:, 0, first : first + width], start=True, stop=True
-            )
+            nc.tensor.matmul(out=bias_ps[:], lhsT=ones[:], rhs=vec_rows[:, 0, bank_cols[c]], start=True, stop=True)
             nc.scalar.copy(out=bias_bc[:, first : first + width], in_=bias_ps[:, :width])
             gain_ps = gain_psum.tile([P, BANK], F32, tag="gain%d" % c)
             nc.tensor.matmul(out=gain_ps[:], lhsT=ones[:], rhs=vec_rows[:, 1, bank_cols[c]], start=True, stop=True)
@@ -155,7 +153,7 @@ def tile_transformerblock_pb_t_kernel(tc, y_act, h, W2, b2, g2, out):
             nc.vector.tensor_tensor(
                 out=resid_of[i][:, GPSIMD_COLS:],
                 in0=h_sb[i // GROUP][:, first + GPSIMD_COLS : first + E],
-                in1=bias_tail[:],
+                in1=bias_last_bank[:, GPSIMD_COLS - (E - BANK) :],
                 op=ALU.add,
             )
 

@@ -25,7 +25,6 @@ N_GROUPS = N_TILES // GROUP
 PAIR = 2
 WORDS = K // 2
 LOADS_AHEAD = 3
-GPSIMD_COLS = 896
 
 FLOPS = 2 * TOKENS * K * E
 
@@ -42,10 +41,11 @@ def tile_transformerblock_pb_t_kernel(tc, y_act, h, W2, b2, g2, out):
         loads = ctx.enter_context(tc.tile_pool(name="loads", bufs=LOADS_AHEAD))
         operand = ctx.enter_context(tc.tile_pool(name="operand", bufs=3))
         rows = ctx.enter_context(tc.tile_pool(name="rows", bufs=6))
+        pairs = ctx.enter_context(tc.tile_pool(name="pairs", bufs=4))
         stats = ctx.enter_context(tc.tile_pool(name="stats", bufs=8))
         gain_psum = ctx.enter_context(tc.psum_pool(name="gain_psum", bufs=1))
         acc_psum = ctx.enter_context(tc.psum_pool(name="acc_psum", bufs=2))
-        xt_psum = ctx.enter_context(tc.psum_pool(name="xt_psum", bufs=1))
+        xt_psum = ctx.enter_context(tc.psum_pool(name="xt_psum", bufs=2))
         ctx.enter_context(tc.manual_schedule())
 
         y_sb, h_sb = {}, {}
@@ -81,16 +81,12 @@ def tile_transformerblock_pb_t_kernel(tc, y_act, h, W2, b2, g2, out):
         ident = consts.tile([P, P], F32)
         make_identity(nc, ident[:])
 
-        bias_bc = consts.tile([P, GPSIMD_COLS], F32)
-        bias_last_bank = gain_psum.tile([P, BANK], F32)
-        nc.tensor.matmul(out=bias_last_bank[:], lhsT=ones[:], rhs=vec_rows[:, 0, E - BANK : E], start=True, stop=True)
+        bias_bc = consts.tile([P, E], F32)
         gain_bc = []
         for c in range(BANKS):
-            first = c * BANK
-            width = min(BANK, GPSIMD_COLS - first)
             bias_ps = acc_psum.tile([P, BANK], F32, tag="acc%d" % c)
             nc.tensor.matmul(out=bias_ps[:], lhsT=ones[:], rhs=vec_rows[:, 0, bank_cols[c]], start=True, stop=True)
-            nc.scalar.copy(out=bias_bc[:, first : first + width], in_=bias_ps[:, :width])
+            nc.scalar.copy(out=bias_bc[:, bank_cols[c]], in_=bias_ps[:])
             gain_ps = gain_psum.tile([P, BANK], F32, tag="gain%d" % c)
             nc.tensor.matmul(out=gain_ps[:], lhsT=ones[:], rhs=vec_rows[:, 1, bank_cols[c]], start=True, stop=True)
             gain_bc.append(gain_ps)
@@ -137,25 +133,17 @@ def tile_transformerblock_pb_t_kernel(tc, y_act, h, W2, b2, g2, out):
             nc.vector.quantize_mx(out=y_codes[:].bitcast(FP8X4), scales=y_scales[:], in_=grouped_of[j][:])
             codes_of[j], scales_of[j] = y_codes, y_scales
 
-        def add_bias(i):
-            resid = rows.tile([P, E], F32)
-            first = (i % GROUP) * E
+        def add_bias_pair(j):
+            resid_pair = pairs.tile([P, PAIR, E], F32)
+            first = (PAIR * j % GROUP) * E
             nc.gpsimd.tensor_tensor(
-                out=resid[:, :GPSIMD_COLS],
-                in0=h_sb[i // GROUP][:, first : first + GPSIMD_COLS],
-                in1=bias_bc[:],
+                out=resid_pair[:],
+                in0=h_sb[PAIR * j // GROUP][:, first : first + PAIR * E].rearrange("p (a e) -> p a e", a=PAIR),
+                in1=bias_bc[:].unsqueeze(1).to_broadcast([P, PAIR, E]),
                 op=ALU.add,
             )
-            resid_of[i] = resid
-
-        def add_bias_tail(i):
-            first = (i % GROUP) * E
-            nc.vector.tensor_tensor(
-                out=resid_of[i][:, GPSIMD_COLS:],
-                in0=h_sb[i // GROUP][:, first + GPSIMD_COLS : first + E],
-                in1=bias_last_bank[:, GPSIMD_COLS - (E - BANK) :],
-                op=ALU.add,
-            )
+            for a in range(PAIR):
+                resid_of[PAIR * j + a] = resid_pair[:, a, :]
 
         def multiply(i):
             tokens = slice((i % PAIR) * P, (i % PAIR + 1) * P)
@@ -241,10 +229,9 @@ def tile_transformerblock_pb_t_kernel(tc, y_act, h, W2, b2, g2, out):
 
         for s in range(-4, N_TILES + 3):
             if_first_of_pair(transpose_pair, s + 4)
-            if_tile(add_bias, s + 3)
+            if_first_of_pair(add_bias_pair, s + 4)
             if_tile(multiply, s + 1)
             if_tile(add_product, s)
-            if_tile(add_bias_tail, s + 1)
             if_first_of_pair(quantise_pair, s + 3)
             if_tile(centre_and_gain, s - 1)
             if_tile(negative_mean, s)
@@ -253,5 +240,5 @@ def tile_transformerblock_pb_t_kernel(tc, y_act, h, W2, b2, g2, out):
             if_tile(normalise_and_store, s - 3)
             if_tile(standard_deviation, s - 1)
             if_first_of_pair(regroup_pair, s + 4)
-            if s > 0 and s % GROUP == GROUP - 1 and s // GROUP + LOADS_AHEAD < N_GROUPS:
+            if s > 0 and s % GROUP == 1 and s // GROUP + LOADS_AHEAD < N_GROUPS:
                 load_group(s // GROUP + LOADS_AHEAD)

@@ -41,7 +41,6 @@ def tile_transformerblock_pb_t_kernel(tc, y_act, h, W2, b2, g2, out):
         loads = ctx.enter_context(tc.tile_pool(name="loads", bufs=LOADS_AHEAD))
         operand = ctx.enter_context(tc.tile_pool(name="operand", bufs=3))
         rows = ctx.enter_context(tc.tile_pool(name="rows", bufs=6))
-        pairs = ctx.enter_context(tc.tile_pool(name="pairs", bufs=4))
         stats = ctx.enter_context(tc.tile_pool(name="stats", bufs=8))
         gain_psum = ctx.enter_context(tc.psum_pool(name="gain_psum", bufs=1))
         acc_psum = ctx.enter_context(tc.psum_pool(name="acc_psum", bufs=2))
@@ -51,7 +50,7 @@ def tile_transformerblock_pb_t_kernel(tc, y_act, h, W2, b2, g2, out):
         y_sb, h_sb = {}, {}
         xt_of, grouped_of, codes_of, scales_of = {}, {}, {}, {}
         acc_of, resid_of, scaled_of = {}, {}, {}
-        sums_of, negmean_of, sumsq_of, std_of, rstd_of = {}, {}, {}, {}, {}
+        sums_of, negmean_of, sumsq_of, rstd_of = {}, {}, {}, {}
 
         def load_group(g):
             y_t = loads.tile([P, GROUP * K], BF16)
@@ -77,7 +76,7 @@ def tile_transformerblock_pb_t_kernel(tc, y_act, h, W2, b2, g2, out):
         eps_col = consts.tile([P, 1], F32)
         nc.vector.memset(eps_col[:], EPS)
         table_warm = consts.tile([P, 1], F32)
-        nc.scalar.activation(out=table_warm[:], in_=eps_col[:], func=ACT.Sqrt)
+        nc.scalar.activation(out=table_warm[:], in_=eps_col[:], func=ACT.Abs_reciprocal_sqrt)
         ident = consts.tile([P, P], F32)
         make_identity(nc, ident[:])
 
@@ -120,40 +119,41 @@ def tile_transformerblock_pb_t_kernel(tc, y_act, h, W2, b2, g2, out):
             xt_of[j] = xt
 
         def regroup_pair(j):
-            grouped = operand.tile([P, PAIR * P * PACK], BF16, align_bytes=64)
+            g = PAIR * j // GROUP
+            if PAIR * j % GROUP == 0:
+                grouped = operand.tile([P, GROUP * P * PACK], BF16, align_bytes=64)
+                grouped_of[g] = grouped
+            first = (PAIR * j % GROUP) * P * PACK
             nc.scalar.copy(
-                out=grouped[:].bitcast(F32).rearrange("p (a r u) -> p a r u", a=PAIR, u=2),
+                out=grouped_of[g][:, first : first + PAIR * P * PACK]
+                .bitcast(F32)
+                .rearrange("p (a r u) -> p a r u", a=PAIR, u=2),
                 in_=xt_of[j][:].rearrange("p (a u) r -> p a r u", u=2),
             )
-            grouped_of[j] = grouped
 
-        def quantise_pair(j):
-            y_codes = operand.tile([P, PAIR * P], U32, align_bytes=64)
-            y_scales = operand.tile([P, PAIR * P], U8, align_bytes=64)
-            nc.vector.quantize_mx(out=y_codes[:].bitcast(FP8X4), scales=y_scales[:], in_=grouped_of[j][:])
-            codes_of[j], scales_of[j] = y_codes, y_scales
+        def quantise_group(g):
+            y_codes = operand.tile([P, GROUP * P], U32, align_bytes=64)
+            y_scales = operand.tile([P, GROUP * P], U8, align_bytes=64)
+            nc.vector.quantize_mx(out=y_codes[:].bitcast(FP8X4), scales=y_scales[:], in_=grouped_of[g][:])
+            codes_of[g], scales_of[g] = y_codes, y_scales
 
-        def add_bias_pair(j):
-            resid_pair = pairs.tile([P, PAIR, E], F32)
-            first = (PAIR * j % GROUP) * E
+        def add_bias(i):
+            resid = rows.tile([P, E], F32)
+            t = i % GROUP
             nc.gpsimd.tensor_tensor(
-                out=resid_pair[:],
-                in0=h_sb[PAIR * j // GROUP][:, first : first + PAIR * E].rearrange("p (a e) -> p a e", a=PAIR),
-                in1=bias_bc[:].unsqueeze(1).to_broadcast([P, PAIR, E]),
-                op=ALU.add,
+                out=resid[:], in0=h_sb[i // GROUP][:, t * E : (t + 1) * E], in1=bias_bc[:], op=ALU.add
             )
-            for a in range(PAIR):
-                resid_of[PAIR * j + a] = resid_pair[:, a, :]
+            resid_of[i] = resid
 
         def multiply(i):
-            tokens = slice((i % PAIR) * P, (i % PAIR + 1) * P)
+            tokens = slice((i % GROUP) * P, (i % GROUP + 1) * P)
             acc_of[i] = []
             for c in range(BANKS):
                 acc = acc_psum.tile([P, BANK], F32, tag="acc%d" % c)
                 nc.tensor.matmul_mx(
                     out=acc[:],
-                    lhsT=codes_of[i // PAIR][:, tokens].bitcast(FP8X4),
-                    lhsT_scale=scales_of[i // PAIR][:, tokens],
+                    lhsT=codes_of[i // GROUP][:, tokens].bitcast(FP8X4),
+                    lhsT_scale=scales_of[i // GROUP][:, tokens],
                     rhs=w_codes[:, bank_cols[c]].bitcast(FP8X4),
                     rhs_scale=w_scales[:, bank_cols[c]],
                     start=True,
@@ -176,10 +176,10 @@ def tile_transformerblock_pb_t_kernel(tc, y_act, h, W2, b2, g2, out):
             sums_of[i] = sums
 
         def negative_mean(i):
+            scaled_sums = stats.tile([P, BANKS], F32)
             negmean = stats.tile([P, 1], F32)
-            sums = sums_of[i]
-            nc.vector.tensor_scalar(
-                out=negmean[:], in0=sums[:, 0:1], scalar1=sums[:, 1:2], scalar2=-1.0 / E, op0=ALU.add, op1=ALU.mult
+            nc.scalar.activation(
+                out=scaled_sums[:], in_=sums_of[i][:], func=ACT.Copy, scale=-1.0 / E, accum_out=negmean[:]
             )
             negmean_of[i] = negmean
 
@@ -204,14 +204,11 @@ def tile_transformerblock_pb_t_kernel(tc, y_act, h, W2, b2, g2, out):
                 )
             scaled_of[i] = scaled
 
-        def standard_deviation(i):
-            std = stats.tile([P, 1], F32)
-            nc.scalar.activation(out=std[:], in_=sumsq_of[i][:], func=ACT.Sqrt, bias=eps_col[:], scale=1.0 / E)
-            std_of[i] = std
-
-        def reciprocal(i):
+        def reciprocal_std(i):
             rstd = stats.tile([P, 1], F32)
-            nc.vector.reciprocal(out=rstd[:], in_=std_of[i][:])
+            nc.scalar.activation(
+                out=rstd[:], in_=sumsq_of[i][:], func=ACT.Abs_reciprocal_sqrt, bias=eps_col[:], scale=1.0 / E
+            )
             rstd_of[i] = rstd
 
         def normalise_and_store(i):
@@ -223,22 +220,21 @@ def tile_transformerblock_pb_t_kernel(tc, y_act, h, W2, b2, g2, out):
             if 0 <= i < N_TILES:
                 stage(i)
 
-        def if_first_of_pair(stage, i):
-            if 0 <= i < N_TILES and i % PAIR == 0:
-                stage(i // PAIR)
+        def if_first_of(tiles, stage, i):
+            if 0 <= i < N_TILES and i % tiles == 0:
+                stage(i // tiles)
 
-        for s in range(-4, N_TILES + 3):
-            if_first_of_pair(transpose_pair, s + 4)
-            if_first_of_pair(add_bias_pair, s + 4)
+        for s in range(-6, N_TILES + 2):
+            if_first_of(PAIR, transpose_pair, s + 6)
+            if_tile(add_bias, s + 3)
             if_tile(multiply, s + 1)
             if_tile(add_product, s)
-            if_first_of_pair(quantise_pair, s + 3)
+            if_first_of(GROUP, quantise_group, s + 3)
             if_tile(centre_and_gain, s - 1)
-            if_tile(negative_mean, s)
-            if_tile(reciprocal, s - 2)
             if_tile(sum_squares, s - 1)
-            if_tile(normalise_and_store, s - 3)
-            if_tile(standard_deviation, s - 1)
-            if_first_of_pair(regroup_pair, s + 4)
+            if_tile(negative_mean, s)
+            if_tile(normalise_and_store, s - 2)
+            if_tile(reciprocal_std, s - 1)
+            if_first_of(PAIR, regroup_pair, s + 6)
             if s > 0 and s % GROUP == 1 and s // GROUP + LOADS_AHEAD < N_GROUPS:
                 load_group(s // GROUP + LOADS_AHEAD)

@@ -25,6 +25,7 @@ N_GROUPS = N_TILES // GROUP
 PAIR = 2
 WORDS = K // 2
 LOADS_AHEAD = 3
+VECTOR_TAIL = 3
 
 FLOPS = 2 * TOKENS * K * E
 
@@ -41,6 +42,7 @@ def tile_transformerblock_pb_t_kernel(tc, y_act, h, W2, b2, g2, out):
         loads = ctx.enter_context(tc.tile_pool(name="loads", bufs=LOADS_AHEAD))
         operand = ctx.enter_context(tc.tile_pool(name="operand", bufs=3))
         rows = ctx.enter_context(tc.tile_pool(name="rows", bufs=6))
+        resids = ctx.enter_context(tc.tile_pool(name="resids", bufs=8))
         stats = ctx.enter_context(tc.tile_pool(name="stats", bufs=8))
         gain_psum = ctx.enter_context(tc.psum_pool(name="gain_psum", bufs=1))
         acc_psum = ctx.enter_context(tc.psum_pool(name="acc_psum", bufs=2))
@@ -52,24 +54,26 @@ def tile_transformerblock_pb_t_kernel(tc, y_act, h, W2, b2, g2, out):
         acc_of, resid_of, scaled_of = {}, {}, {}
         sums_of, negmean_of, sumsq_of, rstd_of = {}, {}, {}, {}
 
-        def load_group(g):
+        def load_group(g, h_pieces):
             y_t = loads.tile([P, GROUP * K], BF16)
             nc.sync.dma_start(out=y_t[:], in_=y_groups[g])
             h_t = loads.tile([P, GROUP * E], BF16)
-            nc.sync.dma_start(out=h_t[:], in_=h_groups[g])
+            width = GROUP * E // h_pieces
+            for first in range(0, GROUP * E, width):
+                nc.sync.dma_start(out=h_t[:, first : first + width], in_=h_groups[g][:, first : first + width])
             y_sb[g], h_sb[g] = y_t, h_t
 
         vec_rows = consts.tile([P, 2, E], BF16)
         nc.vector.memset(vec_rows[:], 0.0)
-        nc.sync.dma_start(out=vec_rows[0:1, 0, :], in_=b2.unsqueeze(0))
-        nc.sync.dma_start(out=vec_rows[0:1, 1, :], in_=g2.unsqueeze(0))
         w_raw = consts.tile([P, PACK, E], BF16)
         nc.sync.dma_start(
             out=w_raw[:].rearrange("p (u e) c -> p u (e c)", e=2),
             in_=W2.rearrange("(u q e) c -> q u (e c)", u=2, e=2),
         )
+        nc.sync.dma_start(out=vec_rows[0:1, 0, :], in_=b2.unsqueeze(0))
+        nc.sync.dma_start(out=vec_rows[0:1, 1, :], in_=g2.unsqueeze(0))
         for g in range(LOADS_AHEAD):
-            load_group(g)
+            load_group(g, h_pieces=2 if g == 0 else 1)
 
         ones = consts.tile([P, P], BF16)
         nc.vector.memset(ones[:], 1.0)
@@ -138,7 +142,7 @@ def tile_transformerblock_pb_t_kernel(tc, y_act, h, W2, b2, g2, out):
             codes_of[g], scales_of[g] = y_codes, y_scales
 
         def add_bias(i):
-            resid = rows.tile([P, E], F32)
+            resid = resids.tile([P, E], F32)
             t = i % GROUP
             nc.gpsimd.tensor_tensor(
                 out=resid[:], in0=h_sb[i // GROUP][:, t * E : (t + 1) * E], in1=bias_bc[:], op=ALU.add
@@ -213,7 +217,12 @@ def tile_transformerblock_pb_t_kernel(tc, y_act, h, W2, b2, g2, out):
 
         def normalise_and_store(i):
             scaled = scaled_of[i]
-            nc.scalar.activation(out=scaled[:], in_=scaled[:], func=ACT.Copy, scale=rstd_of[i][:])
+            if i < N_TILES - VECTOR_TAIL:
+                nc.scalar.activation(out=scaled[:], in_=scaled[:], func=ACT.Copy, scale=rstd_of[i][:])
+            else:
+                nc.vector.tensor_scalar(
+                    out=scaled[:], in0=scaled[:], scalar1=rstd_of[i][:], scalar2=None, op0=ALU.mult
+                )
             nc.sync.dma_start(out=out_groups[i // GROUP][:, i % GROUP, :], in_=scaled[:])
 
         def if_tile(stage, i):
@@ -224,17 +233,17 @@ def tile_transformerblock_pb_t_kernel(tc, y_act, h, W2, b2, g2, out):
             if 0 <= i < N_TILES and i % tiles == 0:
                 stage(i // tiles)
 
-        for s in range(-6, N_TILES + 2):
+        for s in range(-6, N_TILES + 4):
             if_first_of(PAIR, transpose_pair, s + 6)
             if_tile(add_bias, s + 3)
             if_tile(multiply, s + 1)
             if_tile(add_product, s)
             if_first_of(GROUP, quantise_group, s + 3)
-            if_tile(centre_and_gain, s - 1)
-            if_tile(sum_squares, s - 1)
-            if_tile(negative_mean, s)
-            if_tile(normalise_and_store, s - 2)
-            if_tile(reciprocal_std, s - 1)
+            if_tile(centre_and_gain, s - 2)
+            if_tile(sum_squares, s - 2)
+            if_tile(negative_mean, s - 1)
+            if_tile(normalise_and_store, s - 4)
+            if_tile(reciprocal_std, s - 2)
             if_first_of(PAIR, regroup_pair, s + 6)
             if s > 0 and s % GROUP == 1 and s // GROUP + LOADS_AHEAD < N_GROUPS:
-                load_group(s // GROUP + LOADS_AHEAD)
+                load_group(s // GROUP + LOADS_AHEAD, h_pieces=1)

@@ -25,7 +25,6 @@ N_GROUPS = N_TILES // GROUP
 PAIR = 2
 WORDS = K // 2
 LOADS_AHEAD = 3
-VECTOR_TAIL = 3
 
 FLOPS = 2 * TOKENS * K * E
 
@@ -63,33 +62,50 @@ def tile_transformerblock_pb_t_kernel(tc, y_act, h, W2, b2, g2, out):
                 nc.sync.dma_start(out=h_t[:, first : first + width], in_=h_groups[g][:, first : first + width])
             y_sb[g], h_sb[g] = y_t, h_t
 
-        vec_rows = consts.tile([P, 2, E], BF16)
-        nc.vector.memset(vec_rows[:], 0.0)
-        w_raw = consts.tile([P, PACK, E], BF16)
-        nc.sync.dma_start(
-            out=w_raw[:].rearrange("p (u e) c -> p u (e c)", e=2),
-            in_=W2.rearrange("(u q e) c -> q u (e c)", u=2, e=2),
-        )
-        nc.sync.dma_start(out=vec_rows[0:1, 0, :], in_=b2.unsqueeze(0))
-        nc.sync.dma_start(out=vec_rows[0:1, 1, :], in_=g2.unsqueeze(0))
-        for g in range(LOADS_AHEAD):
-            load_group(g, h_pieces=2 if g == 0 else 1)
-
-        ones = consts.tile([P, P], BF16)
-        nc.vector.memset(ones[:], 1.0)
         eps_col = consts.tile([P, 1], F32)
         nc.vector.memset(eps_col[:], EPS)
+        ones = consts.tile([P, P], BF16)
+        nc.vector.memset(ones[:], 1.0)
+        vec_rows = consts.tile([P, 2, E], BF16)
+        nc.vector.memset(vec_rows[:].rearrange("p v e -> p (v e)").bitcast(U32), 0)
         table_warm = consts.tile([P, 1], F32)
         nc.scalar.activation(out=table_warm[:], in_=eps_col[:], func=ACT.Abs_reciprocal_sqrt)
         ident = consts.tile([P, P], F32)
         make_identity(nc, ident[:])
 
+        w_raw = [consts.tile([P, PACK, BANK], BF16, name="w_raw%d" % c) for c in range(BANKS)]
+        w_rows = W2.rearrange("(p t) c -> p t c", t=PACK)
+        y_sb[0] = loads.tile([P, GROUP * K], BF16, name="y_t")
+        h_sb[0] = loads.tile([P, GROUP * E], BF16, name="h_t")
+
+        def load_w(c):
+            nc.sync.dma_start(out=w_raw[c][:], in_=w_rows[:, :, bank_cols[c]])
+
+        def load_y(first, last):
+            nc.sync.dma_start(out=y_sb[0][:, first * K : last * K], in_=y_groups[0][:, first * K : last * K])
+
+        def load_h(first, last):
+            nc.sync.dma_start(out=h_sb[0][:, first * E : last * E], in_=h_groups[0][:, first * E : last * E])
+
+        nc.scalar.dma_start(out=vec_rows[0:1, 0, :], in_=b2.unsqueeze(0))
+        nc.scalar.dma_start(out=vec_rows[0:1, 1, :], in_=g2.unsqueeze(0))
+        load_w(0)
+        load_y(0, 2)
+        load_h(0, 1)
+        load_w(1)
+        load_h(1, 2)
+        load_y(2, 4)
+        load_h(2, 4)
+        for g in range(1, LOADS_AHEAD):
+            load_group(g, h_pieces=1)
+
         bias_bc = consts.tile([P, E], F32)
-        gain_bc = []
         for c in range(BANKS):
             bias_ps = acc_psum.tile([P, BANK], F32, tag="acc%d" % c)
             nc.tensor.matmul(out=bias_ps[:], lhsT=ones[:], rhs=vec_rows[:, 0, bank_cols[c]], start=True, stop=True)
             nc.scalar.copy(out=bias_bc[:, bank_cols[c]], in_=bias_ps[:])
+        gain_bc = []
+        for c in range(BANKS):
             gain_ps = gain_psum.tile([P, BANK], F32, tag="gain%d" % c)
             nc.tensor.matmul(out=gain_ps[:], lhsT=ones[:], rhs=vec_rows[:, 1, bank_cols[c]], start=True, stop=True)
             gain_bc.append(gain_ps)
@@ -97,15 +113,14 @@ def tile_transformerblock_pb_t_kernel(tc, y_act, h, W2, b2, g2, out):
         w_grouped = consts.tile([P, E, PACK], BF16, align_bytes=64)
         w_codes = consts.tile([P, E], U32, align_bytes=64)
         w_scales = consts.tile([P, E], U8, align_bytes=64)
-        nc.vector.tensor_copy(
-            out=w_grouped[:, bank_cols[0], :].rearrange("p (c i) t -> p c t i", i=4),
-            in_=w_raw[:, :, bank_cols[0]].rearrange("p t (c i) -> p c t i", i=4),
-        )
-        nc.scalar.copy(
-            out=w_grouped[:, bank_cols[1], :].rearrange("p (c i) t -> p c t i", i=4),
-            in_=w_raw[:, :, bank_cols[1]].rearrange("p t (c i) -> p c t i", i=4),
-        )
-        for c in range(BANKS):
+
+        def regroup_w(copy, c, first, last):
+            copy(
+                out=w_grouped[:, c * BANK + first : c * BANK + last, :].rearrange("p (c i) t -> p c t i", i=4),
+                in_=w_raw[c][:, :, first:last].rearrange("p t (c i) -> p c t i", i=4),
+            )
+
+        def quantise_w(c):
             nc.vector.quantize_mx(
                 out=w_codes[:, bank_cols[c]].bitcast(FP8X4),
                 scales=w_scales[:, bank_cols[c]],
@@ -118,8 +133,7 @@ def tile_transformerblock_pb_t_kernel(tc, y_act, h, W2, b2, g2, out):
             for a in range(PAIR):
                 t = (PAIR * j + a) % GROUP
                 for u in range(2):
-                    first = t * WORDS + u * P
-                    nc.tensor.transpose(xt[:, 2 * a + u, :], y_words[:, first : first + P], ident[:])
+                    nc.tensor.transpose(xt[:, 2 * a + u, :], y_words[:, t * WORDS + u : (t + 1) * WORDS : 2], ident[:])
             xt_of[j] = xt
 
         def regroup_pair(j):
@@ -135,18 +149,26 @@ def tile_transformerblock_pb_t_kernel(tc, y_act, h, W2, b2, g2, out):
                 in_=xt_of[j][:].rearrange("p (a u) r -> p a r u", u=2),
             )
 
+        def quantise(g, first, last):
+            if first == 0:
+                y_codes = operand.tile([P, GROUP * P], U32, align_bytes=64)
+                y_scales = operand.tile([P, GROUP * P], U8, align_bytes=64)
+                codes_of[g], scales_of[g] = y_codes, y_scales
+            words = slice(first * P, last * P)
+            nc.vector.quantize_mx(
+                out=codes_of[g][:, words].bitcast(FP8X4),
+                scales=scales_of[g][:, words],
+                in_=grouped_of[g][:, first * P * PACK : last * P * PACK],
+            )
+
         def quantise_group(g):
-            y_codes = operand.tile([P, GROUP * P], U32, align_bytes=64)
-            y_scales = operand.tile([P, GROUP * P], U8, align_bytes=64)
-            nc.vector.quantize_mx(out=y_codes[:].bitcast(FP8X4), scales=y_scales[:], in_=grouped_of[g][:])
-            codes_of[g], scales_of[g] = y_codes, y_scales
+            quantise(g, 0, GROUP)
 
         def add_bias(i):
             resid = resids.tile([P, E], F32)
-            t = i % GROUP
-            nc.gpsimd.tensor_tensor(
-                out=resid[:], in0=h_sb[i // GROUP][:, t * E : (t + 1) * E], in1=bias_bc[:], op=ALU.add
-            )
+            h_t = h_sb[i // GROUP][:, i % GROUP * E : (i % GROUP + 1) * E]
+            for cols in bank_cols if i == 0 else [slice(0, E)]:
+                nc.gpsimd.tensor_tensor(out=resid[:, cols], in0=h_t[:, cols], in1=bias_bc[:, cols], op=ALU.add)
             resid_of[i] = resid
 
         def multiply(i):
@@ -215,15 +237,32 @@ def tile_transformerblock_pb_t_kernel(tc, y_act, h, W2, b2, g2, out):
             )
             rstd_of[i] = rstd
 
+        def scale_on_scalar(i, cols):
+            nc.scalar.activation(
+                out=scaled_of[i][:, cols], in_=scaled_of[i][:, cols], func=ACT.Copy, scale=rstd_of[i][:]
+            )
+
+        def scale_on_vector(i, cols):
+            nc.vector.tensor_scalar(
+                out=scaled_of[i][:, cols], in0=scaled_of[i][:, cols], scalar1=rstd_of[i][:], scalar2=None, op0=ALU.mult
+            )
+
+        def scale_on_gpsimd(i, cols):
+            nc.gpsimd.tensor_scalar(
+                out=scaled_of[i][:, cols],
+                in0=scaled_of[i][:, cols],
+                scalar1=rstd_of[i][:],
+                scalar2=0.0,
+                op0=ALU.mult,
+                op1=ALU.add,
+            )
+
+        def scale_and_store(i, scale, cols=slice(0, E)):
+            scale(i, cols)
+            nc.sync.dma_start(out=out_groups[i // GROUP][:, i % GROUP, cols], in_=scaled_of[i][:, cols])
+
         def normalise_and_store(i):
-            scaled = scaled_of[i]
-            if i < N_TILES - VECTOR_TAIL:
-                nc.scalar.activation(out=scaled[:], in_=scaled[:], func=ACT.Copy, scale=rstd_of[i][:])
-            else:
-                nc.vector.tensor_scalar(
-                    out=scaled[:], in0=scaled[:], scalar1=rstd_of[i][:], scalar2=None, op0=ALU.mult
-                )
-            nc.sync.dma_start(out=out_groups[i // GROUP][:, i % GROUP, :], in_=scaled[:])
+            scale_and_store(i, scale_on_scalar)
 
         def if_tile(stage, i):
             if 0 <= i < N_TILES:
@@ -233,12 +272,31 @@ def tile_transformerblock_pb_t_kernel(tc, y_act, h, W2, b2, g2, out):
             if 0 <= i < N_TILES and i % tiles == 0:
                 stage(i // tiles)
 
-        for s in range(-6, N_TILES + 4):
+        transpose_pair(0)
+        transpose_pair(1)
+        regroup_w(nc.vector.tensor_copy, 0, 0, BANK)
+        regroup_pair(0)
+        regroup_w(nc.vector.tensor_copy, 1, 0, BANK // 2)
+        regroup_w(nc.scalar.copy, 1, BANK // 2, BANK)
+        quantise_w(0)
+        quantise(0, 0, 2)
+        quantise_w(1)
+        regroup_pair(1)
+        add_bias(0)
+        multiply(0)
+        add_bias(1)
+        add_bias(2)
+        transpose_pair(2)
+        regroup_pair(2)
+        for s in range(N_TILES - 1):
             if_first_of(PAIR, transpose_pair, s + 6)
             if_tile(add_bias, s + 3)
             if_tile(multiply, s + 1)
-            if_tile(add_product, s)
-            if_first_of(GROUP, quantise_group, s + 3)
+            add_product(s)
+            if s == 0:
+                quantise(0, 2, 4)
+            else:
+                if_first_of(GROUP, quantise_group, s + 3)
             if_tile(centre_and_gain, s - 2)
             if_tile(sum_squares, s - 2)
             if_tile(negative_mean, s - 1)
@@ -247,3 +305,22 @@ def tile_transformerblock_pb_t_kernel(tc, y_act, h, W2, b2, g2, out):
             if_first_of(PAIR, regroup_pair, s + 6)
             if s > 0 and s % GROUP == 1 and s // GROUP + LOADS_AHEAD < N_GROUPS:
                 load_group(s // GROUP + LOADS_AHEAD, h_pieces=1)
+        last = N_TILES - 1
+        centre_and_gain(last - 2)
+        add_product(last)
+        sum_squares(last - 2)
+        negative_mean(last - 1)
+        reciprocal_std(last - 2)
+        scale_and_store(last - 4, scale_on_gpsimd)
+        sum_squares(last - 1)
+        centre_and_gain(last - 1)
+        negative_mean(last)
+        reciprocal_std(last - 1)
+        scale_and_store(last - 3, scale_on_gpsimd)
+        scale_and_store(last - 2, scale_on_gpsimd)
+        sum_squares(last)
+        centre_and_gain(last)
+        reciprocal_std(last)
+        scale_and_store(last - 1, scale_on_gpsimd)
+        scale_and_store(last, scale_on_scalar, bank_cols[0])
+        scale_and_store(last, scale_on_vector, bank_cols[1])

@@ -64,10 +64,12 @@ def tile_transformerblock_pb_t_kernel(tc, y_act, h, W2, b2, g2, out):
 
         eps_col = consts.tile([P, 1], F32)
         nc.vector.memset(eps_col[:], EPS)
+        b2_rows = consts.tile([P, E], BF16)
+        nc.vector.memset(b2_rows[:].bitcast(U32), 0)
         ones = consts.tile([P, P], BF16)
         nc.vector.memset(ones[:], 1.0)
-        vec_rows = consts.tile([P, 2, E], BF16)
-        nc.vector.memset(vec_rows[:].rearrange("p v e -> p (v e)").bitcast(U32), 0)
+        g2_rows = consts.tile([P, E], BF16)
+        nc.vector.memset(g2_rows[:].bitcast(U32), 0)
         table_warm = consts.tile([P, 1], F32)
         nc.scalar.activation(out=table_warm[:], in_=eps_col[:], func=ACT.Abs_reciprocal_sqrt)
         ident = consts.tile([P, P], F32)
@@ -87,12 +89,12 @@ def tile_transformerblock_pb_t_kernel(tc, y_act, h, W2, b2, g2, out):
         def load_h(first, last):
             nc.sync.dma_start(out=h_sb[0][:, first * E : last * E], in_=h_groups[0][:, first * E : last * E])
 
-        nc.scalar.dma_start(out=vec_rows[0:1, 0, :], in_=b2.unsqueeze(0))
-        nc.scalar.dma_start(out=vec_rows[0:1, 1, :], in_=g2.unsqueeze(0))
+        nc.sync.dma_start(out=b2_rows[0:1, :], in_=b2.unsqueeze(0))
         load_w(0)
-        load_y(0, 2)
         load_h(0, 1)
+        load_y(0, 2)
         load_w(1)
+        nc.sync.dma_start(out=g2_rows[0:1, :], in_=g2.unsqueeze(0))
         load_h(1, 2)
         load_y(2, 4)
         load_h(2, 4)
@@ -102,14 +104,8 @@ def tile_transformerblock_pb_t_kernel(tc, y_act, h, W2, b2, g2, out):
         bias_bc = consts.tile([P, E], F32)
         for c in range(BANKS):
             bias_ps = acc_psum.tile([P, BANK], F32, tag="acc%d" % c)
-            nc.tensor.matmul(out=bias_ps[:], lhsT=ones[:], rhs=vec_rows[:, 0, bank_cols[c]], start=True, stop=True)
+            nc.tensor.matmul(out=bias_ps[:], lhsT=ones[:], rhs=b2_rows[:, bank_cols[c]], start=True, stop=True)
             nc.scalar.copy(out=bias_bc[:, bank_cols[c]], in_=bias_ps[:])
-        gain_bc = []
-        for c in range(BANKS):
-            gain_ps = gain_psum.tile([P, BANK], F32, tag="gain%d" % c)
-            nc.tensor.matmul(out=gain_ps[:], lhsT=ones[:], rhs=vec_rows[:, 1, bank_cols[c]], start=True, stop=True)
-            gain_bc.append(gain_ps)
-
         w_grouped = consts.tile([P, E, PACK], BF16, align_bytes=64)
         w_codes = consts.tile([P, E], U32, align_bytes=64)
         w_scales = consts.tile([P, E], U8, align_bytes=64)
@@ -273,6 +269,11 @@ def tile_transformerblock_pb_t_kernel(tc, y_act, h, W2, b2, g2, out):
                 stage(i // tiles)
 
         transpose_pair(0)
+        gain_bc = []
+        for c in range(BANKS):
+            gain_ps = gain_psum.tile([P, BANK], F32, tag="gain%d" % c)
+            nc.tensor.matmul(out=gain_ps[:], lhsT=ones[:], rhs=g2_rows[:, bank_cols[c]], start=True, stop=True)
+            gain_bc.append(gain_ps)
         transpose_pair(1)
         regroup_w(nc.vector.tensor_copy, 0, 0, BANK)
         regroup_pair(0)

@@ -40,7 +40,7 @@ def tile_transformerblock_pb_t_kernel(tc, y_act, h, W2, b2, g2, out):
         consts = ctx.enter_context(tc.tile_pool(name="consts", bufs=1))
         loads = ctx.enter_context(tc.tile_pool(name="loads", bufs=LOADS_AHEAD))
         operand = ctx.enter_context(tc.tile_pool(name="operand", bufs=3))
-        rows = ctx.enter_context(tc.tile_pool(name="rows", bufs=6))
+        rows = ctx.enter_context(tc.tile_pool(name="rows", bufs=8))
         resids = ctx.enter_context(tc.tile_pool(name="resids", bufs=8))
         stats = ctx.enter_context(tc.tile_pool(name="stats", bufs=8))
         gain_psum = ctx.enter_context(tc.psum_pool(name="gain_psum", bufs=1))
@@ -65,7 +65,7 @@ def tile_transformerblock_pb_t_kernel(tc, y_act, h, W2, b2, g2, out):
         eps_col = consts.tile([P, 1], F32)
         nc.vector.memset(eps_col[:], EPS)
         b2_rows = consts.tile([P, E], BF16)
-        nc.vector.memset(b2_rows[:].bitcast(U32), 0)
+        nc.gpsimd.memset(b2_rows[:].bitcast(U32), 0)
         ones = consts.tile([P, P], BF16)
         nc.vector.memset(ones[:], 1.0)
         g2_rows = consts.tile([P, E], BF16)
@@ -89,8 +89,8 @@ def tile_transformerblock_pb_t_kernel(tc, y_act, h, W2, b2, g2, out):
         def load_h(first, last):
             nc.sync.dma_start(out=h_sb[0][:, first * E : last * E], in_=h_groups[0][:, first * E : last * E])
 
-        nc.sync.dma_start(out=b2_rows[0:1, :], in_=b2.unsqueeze(0))
         load_w(0)
+        nc.sync.dma_start(out=b2_rows[0:1, :], in_=b2.unsqueeze(0))
         load_h(0, 1)
         load_y(0, 2)
         load_w(1)
@@ -215,15 +215,14 @@ def tile_transformerblock_pb_t_kernel(tc, y_act, h, W2, b2, g2, out):
 
         def centre_and_gain(i):
             scaled = rows.tile([P, E], F32)
-            for c in range(BANKS):
-                nc.vector.scalar_tensor_tensor(
-                    out=scaled[:, bank_cols[c]],
-                    in0=resid_of[i][:, bank_cols[c]],
-                    scalar=negmean_of[i][:],
-                    in1=gain_bc[c][:],
-                    op0=ALU.add,
-                    op1=ALU.mult,
-                )
+            nc.vector.scalar_tensor_tensor(
+                out=scaled[:],
+                in0=resid_of[i][:],
+                scalar=negmean_of[i][:],
+                in1=gain_bc[:],
+                op0=ALU.add,
+                op1=ALU.mult,
+            )
             scaled_of[i] = scaled
 
         def reciprocal_std(i):
@@ -269,17 +268,14 @@ def tile_transformerblock_pb_t_kernel(tc, y_act, h, W2, b2, g2, out):
                 stage(i // tiles)
 
         transpose_pair(0)
-        gain_bc = []
+        gain_bc = gain_psum.tile([P, E], BF16)
         for c in range(BANKS):
-            gain_ps = gain_psum.tile([P, BANK], F32, tag="gain%d" % c)
-            nc.tensor.matmul(out=gain_ps[:], lhsT=ones[:], rhs=g2_rows[:, bank_cols[c]], start=True, stop=True)
-            gain_bc.append(gain_ps)
+            nc.tensor.matmul(out=gain_bc[:, bank_cols[c]], lhsT=ones[:], rhs=g2_rows[:, bank_cols[c]], start=True, stop=True)
         transpose_pair(1)
         regroup_w(nc.vector.tensor_copy, 0, 0, BANK)
         regroup_pair(0)
-        regroup_w(nc.vector.tensor_copy, 1, 0, BANK // 2)
-        regroup_w(nc.scalar.copy, 1, BANK // 2, BANK)
         quantise_w(0)
+        regroup_w(nc.vector.tensor_copy, 1, 0, BANK)
         quantise(0, 0, 2)
         quantise_w(1)
         regroup_pair(1)

from contextlib import ExitStack

import concourse.mybir as mybir
from concourse.masks import make_identity

F32 = mybir.dt.float32
BF16 = mybir.dt.bfloat16
U32 = mybir.dt.uint32
U8 = mybir.dt.uint8
FP8X4 = mybir.dt.float8_e4m3fn_x4
ALU = mybir.AluOpType
ACT = mybir.ActivationFunctionType

P = 128
PACK = 4
TOKENS = 4 * 1024
K = 512
E = 1024
EPS = 1e-5
BANK = 512
BANKS = E // BANK
N_TILES = TOKENS // P
GROUP = 4
N_GROUPS = N_TILES // GROUP
PAIR = 2
WORDS = K // 2
LOADS_AHEAD = 3

FLOPS = 2 * TOKENS * K * E


def tile_transformerblock_pb_t_kernel(tc, y_act, h, W2, b2, g2, out):
    nc = tc.nc
    y_groups = y_act.flatten_outer_dims().rearrange("(g p t) k -> g p (t k)", p=P, t=GROUP)
    h_groups = h.flatten_outer_dims().rearrange("(g p t) e -> g p (t e)", p=P, t=GROUP)
    out_groups = out.flatten_outer_dims().rearrange("(g p t) e -> g p t e", p=P, t=GROUP)
    bank_cols = [slice(c * BANK, (c + 1) * BANK) for c in range(BANKS)]

    with ExitStack() as ctx:
        consts = ctx.enter_context(tc.tile_pool(name="consts", bufs=1))
        loads = ctx.enter_context(tc.tile_pool(name="loads", bufs=LOADS_AHEAD))
        operand = ctx.enter_context(tc.tile_pool(name="operand", bufs=3))
        rows = ctx.enter_context(tc.tile_pool(name="rows", bufs=8))
        resids = ctx.enter_context(tc.tile_pool(name="resids", bufs=8))
        stats = ctx.enter_context(tc.tile_pool(name="stats", bufs=8))
        gain_psum = ctx.enter_context(tc.psum_pool(name="gain_psum", bufs=1))
        acc_psum = ctx.enter_context(tc.psum_pool(name="acc_psum", bufs=2))
        xt_psum = ctx.enter_context(tc.psum_pool(name="xt_psum", bufs=2))
        ctx.enter_context(tc.manual_schedule())

        y_sb, h_sb = {}, {}
        xt_of, grouped_of, codes_of, scales_of = {}, {}, {}, {}
        acc_of, resid_of, scaled_of = {}, {}, {}
        sums_of, negmean_of, sumsq_of, rstd_of = {}, {}, {}, {}

        def load_group(g, h_pieces):
            y_t = loads.tile([P, GROUP * K], BF16)
            nc.sync.dma_start(out=y_t[:], in_=y_groups[g])
            h_t = loads.tile([P, GROUP * E], BF16)
            width = GROUP * E // h_pieces
            for first in range(0, GROUP * E, width):
                nc.sync.dma_start(out=h_t[:, first : first + width], in_=h_groups[g][:, first : first + width])
            y_sb[g], h_sb[g] = y_t, h_t

        eps_col = consts.tile([P, 1], F32)
        nc.vector.memset(eps_col[:], EPS)
        b2_rows = consts.tile([P, E], BF16)
        nc.gpsimd.memset(b2_rows[:].bitcast(U32), 0)
        ones = consts.tile([P, P], BF16)
        nc.vector.memset(ones[:], 1.0)
        g2_rows = consts.tile([P, E], BF16)
        nc.vector.memset(g2_rows[:].bitcast(U32), 0)
        table_warm = consts.tile([P, 1], F32)
        nc.scalar.activation(out=table_warm[:], in_=eps_col[:], func=ACT.Abs_reciprocal_sqrt)
        ident = consts.tile([P, P], F32)
        make_identity(nc, ident[:])

        w_raw = [consts.tile([P, PACK, BANK], BF16, name="w_raw%d" % c) for c in range(BANKS)]
        w_rows = W2.rearrange("(p t) c -> p t c", t=PACK)
        y_sb[0] = loads.tile([P, GROUP * K], BF16, name="y_t")
        h_sb[0] = loads.tile([P, GROUP * E], BF16, name="h_t")

        def load_w(c):
            nc.sync.dma_start(out=w_raw[c][:], in_=w_rows[:, :, bank_cols[c]])

        def load_y(first, last):
            nc.sync.dma_start(out=y_sb[0][:, first * K : last * K], in_=y_groups[0][:, first * K : last * K])

        def load_h(first, last):
            nc.sync.dma_start(out=h_sb[0][:, first * E : last * E], in_=h_groups[0][:, first * E : last * E])

        load_w(0)
        nc.sync.dma_start(out=b2_rows[0:1, :], in_=b2.unsqueeze(0))
        load_h(0, 1)
        load_y(0, 2)
        load_w(1)
        nc.sync.dma_start(out=g2_rows[0:1, :], in_=g2.unsqueeze(0))
        load_h(1, 2)
        load_y(2, 4)
        load_h(2, 4)
        for g in range(1, LOADS_AHEAD):
            load_group(g, h_pieces=1)

        bias_bc = consts.tile([P, E], F32)
        for c in range(BANKS):
            bias_ps = acc_psum.tile([P, BANK], F32, tag="acc%d" % c)
            nc.tensor.matmul(out=bias_ps[:], lhsT=ones[:], rhs=b2_rows[:, bank_cols[c]], start=True, stop=True)
            nc.scalar.copy(out=bias_bc[:, bank_cols[c]], in_=bias_ps[:])
        w_grouped = consts.tile([P, E, PACK], BF16, align_bytes=64)
        w_codes = consts.tile([P, E], U32, align_bytes=64)
        w_scales = consts.tile([P, E], U8, align_bytes=64)

        def regroup_w(copy, c, first, last):
            copy(
                out=w_grouped[:, c * BANK + first : c * BANK + last, :].rearrange("p (c i) t -> p c t i", i=4),
                in_=w_raw[c][:, :, first:last].rearrange("p t (c i) -> p c t i", i=4),
            )

        def quantise_w(c):
            nc.vector.quantize_mx(
                out=w_codes[:, bank_cols[c]].bitcast(FP8X4),
                scales=w_scales[:, bank_cols[c]],
                in_=w_grouped[:, bank_cols[c], :].rearrange("p c t -> p (c t)"),
            )

        def transpose_pair(j):
            y_words = y_sb[PAIR * j // GROUP][:].bitcast(F32)
            xt = xt_psum.tile([P, PAIR * 2, P], F32)
            for a in range(PAIR):
                t = (PAIR * j + a) % GROUP
                for u in range(2):
                    nc.tensor.transpose(xt[:, 2 * a + u, :], y_words[:, t * WORDS + u : (t + 1) * WORDS : 2], ident[:])
            xt_of[j] = xt

        def regroup_pair(j):
            g = PAIR * j // GROUP
            if PAIR * j % GROUP == 0:
                grouped = operand.tile([P, GROUP * P * PACK], BF16, align_bytes=64)
                grouped_of[g] = grouped
            first = (PAIR * j % GROUP) * P * PACK
            nc.scalar.copy(
                out=grouped_of[g][:, first : first + PAIR * P * PACK]
                .bitcast(F32)
                .rearrange("p (a r u) -> p a r u", a=PAIR, u=2),
                in_=xt_of[j][:].rearrange("p (a u) r -> p a r u", u=2),
            )

        def quantise(g, first, last):
            if first == 0:
                y_codes = operand.tile([P, GROUP * P], U32, align_bytes=64)
                y_scales = operand.tile([P, GROUP * P], U8, align_bytes=64)
                codes_of[g], scales_of[g] = y_codes, y_scales
            words = slice(first * P, last * P)
            nc.vector.quantize_mx(
                out=codes_of[g][:, words].bitcast(FP8X4),
                scales=scales_of[g][:, words],
                in_=grouped_of[g][:, first * P * PACK : last * P * PACK],
            )

        def quantise_group(g):
            quantise(g, 0, GROUP)

        def add_bias(i):
            resid = resids.tile([P, E], F32)
            h_t = h_sb[i // GROUP][:, i % GROUP * E : (i % GROUP + 1) * E]
            for cols in bank_cols if i == 0 else [slice(0, E)]:
                nc.gpsimd.tensor_tensor(out=resid[:, cols], in0=h_t[:, cols], in1=bias_bc[:, cols], op=ALU.add)
            resid_of[i] = resid

        def multiply(i):
            tokens = slice((i % GROUP) * P, (i % GROUP + 1) * P)
            acc_of[i] = []
            for c in range(BANKS):
                acc = acc_psum.tile([P, BANK], F32, tag="acc%d" % c)
                nc.tensor.matmul_mx(
                    out=acc[:],
                    lhsT=codes_of[i // GROUP][:, tokens].bitcast(FP8X4),
                    lhsT_scale=scales_of[i // GROUP][:, tokens],
                    rhs=w_codes[:, bank_cols[c]].bitcast(FP8X4),
                    rhs_scale=w_scales[:, bank_cols[c]],
                    start=True,
                    stop=True,
                )
                acc_of[i].append(acc)

        def add_product(i):
            sums = stats.tile([P, BANKS], F32)
            for c, acc in enumerate(acc_of[i]):
                nc.vector.scalar_tensor_tensor(
                    out=resid_of[i][:, bank_cols[c]],
                    in0=resid_of[i][:, bank_cols[c]],
                    scalar=0.0,
                    in1=acc[:],
                    op0=ALU.add,
                    op1=ALU.add,
                    accum_out=sums[:, c : c + 1],
                )
            sums_of[i] = sums

        def negative_mean(i):
            scaled_sums = stats.tile([P, BANKS], F32)
            negmean = stats.tile([P, 1], F32)
            nc.scalar.activation(
                out=scaled_sums[:], in_=sums_of[i][:], func=ACT.Copy, scale=-1.0 / E, accum_out=negmean[:]
            )
            negmean_of[i] = negmean

        def sum_squares(i):
            squares = rows.tile([P, E], BF16, bufs=2)
            sumsq = stats.tile([P, 1], F32)
            nc.scalar.activation(
                out=squares[:], in_=resid_of[i][:], func=ACT.Square, bias=negmean_of[i][:], scale=1.0, accum_out=sumsq[:]
            )
            sumsq_of[i] = sumsq

        def centre_and_gain(i):
            scaled = rows.tile([P, E], F32)
            nc.vector.scalar_tensor_tensor(
                out=scaled[:],
                in0=resid_of[i][:],
                scalar=negmean_of[i][:],
                in1=gain_bc[:],
                op0=ALU.add,
                op1=ALU.mult,
            )
            scaled_of[i] = scaled

        def reciprocal_std(i):
            rstd = stats.tile([P, 1], F32)
            nc.scalar.activation(
                out=rstd[:], in_=sumsq_of[i][:], func=ACT.Abs_reciprocal_sqrt, bias=eps_col[:], scale=1.0 / E
            )
            rstd_of[i] = rstd

        def scale_on_scalar(i, cols):
            nc.scalar.activation(
                out=scaled_of[i][:, cols], in_=scaled_of[i][:, cols], func=ACT.Copy, scale=rstd_of[i][:]
            )

        def scale_on_vector(i, cols):
            nc.vector.tensor_scalar(
                out=scaled_of[i][:, cols], in0=scaled_of[i][:, cols], scalar1=rstd_of[i][:], scalar2=None, op0=ALU.mult
            )

        def scale_on_gpsimd(i, cols):
            nc.gpsimd.tensor_scalar(
                out=scaled_of[i][:, cols],
                in0=scaled_of[i][:, cols],
                scalar1=rstd_of[i][:],
                scalar2=0.0,
                op0=ALU.mult,
                op1=ALU.add,
            )

        def scale_and_store(i, scale, cols=slice(0, E)):
            scale(i, cols)
            nc.sync.dma_start(out=out_groups[i // GROUP][:, i % GROUP, cols], in_=scaled_of[i][:, cols])

        def normalise_and_store(i):
            scale_and_store(i, scale_on_scalar)

        def if_tile(stage, i):
            if 0 <= i < N_TILES:
                stage(i)

        def if_first_of(tiles, stage, i):
            if 0 <= i < N_TILES and i % tiles == 0:
                stage(i // tiles)

        transpose_pair(0)
        gain_bc = gain_psum.tile([P, E], BF16)
        for c in range(BANKS):
            nc.tensor.matmul(out=gain_bc[:, bank_cols[c]], lhsT=ones[:], rhs=g2_rows[:, bank_cols[c]], start=True, stop=True)
        transpose_pair(1)
        regroup_w(nc.vector.tensor_copy, 0, 0, BANK)
        regroup_pair(0)
        quantise_w(0)
        regroup_w(nc.vector.tensor_copy, 1, 0, BANK)
        quantise(0, 0, 2)
        quantise_w(1)
        regroup_pair(1)
        add_bias(0)
        multiply(0)
        add_bias(1)
        add_bias(2)
        transpose_pair(2)
        regroup_pair(2)
        for s in range(N_TILES - 1):
            if_first_of(PAIR, transpose_pair, s + 6)
            if_tile(add_bias, s + 3)
            if_tile(multiply, s + 1)
            add_product(s)
            if s == 0:
                quantise(0, 2, 4)
            else:
                if_first_of(GROUP, quantise_group, s + 3)
            if_tile(centre_and_gain, s - 2)
            if_tile(sum_squares, s - 2)
            if_tile(negative_mean, s - 1)
            if_tile(normalise_and_store, s - 4)
            if_tile(reciprocal_std, s - 2)
            if_first_of(PAIR, regroup_pair, s + 6)
            if s > 0 and s % GROUP == 1 and s // GROUP + LOADS_AHEAD < N_GROUPS:
                load_group(s // GROUP + LOADS_AHEAD, h_pieces=1)
        last = N_TILES - 1
        centre_and_gain(last - 2)
        add_product(last)
        sum_squares(last - 2)
        negative_mean(last - 1)
        reciprocal_std(last - 2)
        scale_and_store(last - 4, scale_on_gpsimd)
        sum_squares(last - 1)
        centre_and_gain(last - 1)
        negative_mean(last)
        reciprocal_std(last - 1)
        scale_and_store(last - 3, scale_on_gpsimd)
        scale_and_store(last - 2, scale_on_gpsimd)
        sum_squares(last)
        centre_and_gain(last)
        reciprocal_std(last)
        scale_and_store(last - 1, scale_on_gpsimd)
        scale_and_store(last, scale_on_scalar, bank_cols[0])
        scale_and_store(last, scale_on_vector, bank_cols[1])
